import numpy as np
import ml_dtypes


BF16 = ml_dtypes.bfloat16


def bf(x):
    return np.asarray(x, np.float32).astype(BF16)


def f64(x):
    return np.asarray(x).astype(np.float64)


E2M1 = np.array([0.0, 0.5, 1.0, 1.5, 2.0, 3.0, 4.0, 6.0, -0.0, -0.5, -1.0, -1.5, -2.0, -3.0, -4.0, -6.0])


def pack_weight(w, fmt):
    k, n = w.shape
    w = f64(bf(w)).reshape(k // 32, 32, n)
    amax = np.abs(w).max(1)
    if fmt == "e4m3":
        byte = np.frexp(amax)[1] - 1 + 127 - 7
    else:
        mant, ex = np.frexp(amax / 6.0)
        byte = np.where(mant > 0.5, ex, ex - 1) + 127
    byte = np.clip(np.where(amax > 0, byte, 1), 1, 254)
    scaled = (w * np.exp2(127.0 - byte)[:, None, :]).reshape(k, n).astype(np.float32)
    by_word = np.ascontiguousarray(scaled.reshape(k // 512, 128, 4, n).transpose(0, 1, 3, 2))
    if fmt == "e4m3":
        words = by_word.astype(ml_dtypes.float8_e4m3fn).view(np.uint8)
    else:
        c = by_word.astype(ml_dtypes.float4_e2m1fn).view(np.uint8) & 0xF
        words = c[..., 0::2] | (c[..., 1::2] << 4)
    return np.ascontiguousarray(words), np.ascontiguousarray(byte.astype(np.uint8).reshape(k // 512, 16, n))


def unpack_weight(words, scales, fmt):
    g, p, n, _ = words.shape
    if fmt == "e4m3":
        vals = np.ascontiguousarray(words).view(ml_dtypes.float8_e4m3fn).astype(np.float64)
    else:
        nib = np.empty((g, p, n, 4), np.uint8)
        nib[..., 0::2] = words & 0xF
        nib[..., 1::2] = words >> 4
        vals = E2M1[nib]
    vals = vals * np.repeat(np.exp2(scales.astype(np.float64) - 127.0), 8, axis=1)[..., None]
    return vals.transpose(0, 1, 3, 2).reshape(g * 512, n)

def pack4(w):
    words, scales = pack_weight(w, "e2m1")
    return words.reshape(words.shape[0], 128, -1), scales


def unpack4(words, scales):
    return unpack_weight(words.reshape(words.shape[0], 128, -1, 2), scales, "e2m1")


def kspread(k):
    return np.exp2(np.repeat(np.random.randint(-6, 7, k // 32), 32).astype(np.float64))


B, T, C, H, KV, HD = 4, 1024, 2048, 16, 4, 128
NQ = H * HD
NK = KV * HD
HALF = HD // 2
ROPE_THETA = 10000.0


def apply_rope(u, cos, sin):
    ur = u.reshape(*u.shape[:-1], HALF, 2)
    ue, uo = ur[..., 0], ur[..., 1]
    c = cos[None, :, None, :]
    s = sin[None, :, None, :]
    out_e = ue * c - uo * s
    out_o = ue * s + uo * c
    return np.stack([out_e, out_o], axis=-1).reshape(u.shape)


def setup_inputs():
    s = kspread(C)
    inv_freq = 1.0 / ROPE_THETA ** (np.arange(0, HD, 2) / HD)
    angles = np.arange(T)[:, None] * inv_freq[None, :]
    x = np.random.standard_normal((B, T, C)) * s
    x_words, x_scales = pack4(np.ascontiguousarray(x.reshape(B * T, C).T))
    w = np.random.standard_normal((NQ + NK + NK, C)) / np.sqrt(C) / s[None, :]
    words, scales = pack4(np.ascontiguousarray(w.T))
    return {"x_words": x_words,
            "x_scales": x_scales,
            "w_qkv_words": words,
            "w_qkv_scales": scales,
            "freqs_cos": bf(np.cos(angles)),
            "freqs_sin": bf(np.sin(angles))}


def reference(x_words, x_scales, w_qkv_words, w_qkv_scales, freqs_cos, freqs_sin):
    cos, sin = f64(freqs_cos), f64(freqs_sin)
    xq = unpack4(x_words, x_scales).T.reshape(B, T, C)
    qkv = xq @ unpack4(w_qkv_words, w_qkv_scales)
    q = qkv[..., :NQ].reshape(B, T, H, HD)
    k = qkv[..., NQ:NQ + NK].reshape(B, T, KV, HD)
    v = qkv[..., NQ + NK:].reshape(B, T, KV, HD)
    return apply_rope(q, cos, sin), apply_rope(k, cos, sin), v

@@ -1,0 +1,172 @@
+from contextlib import ExitStack
+
+import concourse.mybir as mybir
+
+F32 = mybir.dt.float32
+BF16 = mybir.dt.bfloat16
+I32 = mybir.dt.int32
+U8 = mybir.dt.uint8
+FP4X4 = mybir.dt.float4_e2m1fn_x4
+MULT = mybir.AluOpType.mult
+ADD = mybir.AluOpType.add
+
+P = 128
+TOKENS = 4096
+K = 2048
+PASSES = K // 512
+NQ = 2048
+NKV = 512
+NCOLS = NQ + 2 * NKV
+BLOCK = 512
+NBLOCKS = NCOLS // BLOCK
+VBLOCK = 5
+GROUP = 4
+NGROUPS = TOKENS // (P * GROUP)
+HD = 128
+HEADS = BLOCK // HD
+POS_TILES = 1024 // P
+ROTATED = (0, 1, 2, 3, 4)
+V_PLACE = (0, 1, 1, 2, 3, 4, 4, 5)
+
+FLOPS = 2 * TOKENS * K * NCOLS
+
+
+def tile_causalselfattention_pa_kernel(
+    tc, x_words, x_scales, w_qkv_words, w_qkv_scales, freqs_cos, freqs_sin, out_0, out_1, out_2
+):
+    nc = tc.nc
+    q_rows = out_0.rearrange("b t h d -> (b t) (h d)")
+    k_rows = out_1.rearrange("b t h d -> (b t) (h d)")
+    v_rows = out_2.rearrange("b t h d -> (b t) (h d)")
+
+    with ExitStack() as ctx:
+        keep = ctx.enter_context(tc.tile_pool(name="keep", bufs=1))
+        work = ctx.enter_context(tc.tile_pool(name="work", bufs=1))
+        psum = ctx.enter_context(tc.psum_pool(name="psum", bufs=8))
+        ctx.enter_context(tc.manual_schedule())
+
+        x_codes = [keep.tile([P, PASSES, 2 * BLOCK], U8, name="xc%d" % c, align_bytes=64) for c in range(NGROUPS)]
+        x_planes = [keep.tile([P, PASSES, BLOCK], U8, name="xs%d" % c, align_bytes=64) for c in range(NGROUPS)]
+        w_codes = [keep.tile([P, PASSES, 2 * BLOCK], U8, name="wc%d" % n, align_bytes=64) for n in range(NBLOCKS)]
+        w_planes = [keep.tile([P, PASSES, BLOCK], U8, name="ws%d" % n, align_bytes=64) for n in range(NBLOCKS)]
+        cos_raw = keep.tile([P, POS_TILES, HD // 2], BF16, name="cos_raw")
+        sin_raw = keep.tile([P, POS_TILES, HD // 2], BF16, name="sin_raw")
+        cos_tab = keep.tile([P, POS_TILES, HD // 2, 2], F32, name="cos_tab")
+        sin_tab = keep.tile([P, POS_TILES, HD // 2, 2], F32, name="sin_tab")
+
+        def zero_plane(plane):
+            nc.vector.memset(plane[:].bitcast(I32), 0)
+
+        def load_scales(plane, scales, i):
+            for quad in range(4):
+                nc.sync.dma_start(
+                    out=plane[32 * quad : 32 * quad + 4, :, :].bitcast(I32),
+                    in_=scales[:, 4 * quad : 4 * quad + 4, BLOCK * i : BLOCK * (i + 1)]
+                    .rearrange("g r n -> r g n")
+                    .bitcast(I32),
+                )
+
+        def load_codes(codes, words, i, pieces):
+            step = PASSES // pieces
+            for g0 in range(0, PASSES, step):
+                nc.sync.dma_start(
+                    out=codes[:, g0 : g0 + step, :].bitcast(I32),
+                    in_=words[g0 : g0 + step, :, 2 * BLOCK * i : 2 * BLOCK * (i + 1)]
+                    .rearrange("g p b -> p g b")
+                    .bitcast(I32),
+                )
+
+        zero_plane(w_planes[VBLOCK])
+        zero_plane(x_planes[0])
+        load_scales(w_planes[VBLOCK], w_qkv_scales, VBLOCK)
+        load_scales(x_planes[0], x_scales, 0)
+        load_codes(x_codes[0], x_words, 0, 2)
+        load_codes(w_codes[VBLOCK], w_qkv_words, VBLOCK, 2)
+        nc.scalar.dma_start(out=cos_raw[:], in_=freqs_cos.rearrange("(a p) j -> p a j", p=P))
+        nc.scalar.dma_start(out=sin_raw[:], in_=freqs_sin.rearrange("(a p) j -> p a j", p=P))
+        for n in range(VBLOCK):
+            zero_plane(w_planes[n])
+        for c in range(1, NGROUPS):
+            zero_plane(x_planes[c])
+        load_scales(w_planes[0], w_qkv_scales, 0)
+        load_scales(w_planes[1], w_qkv_scales, 1)
+        load_codes(w_codes[0], w_qkv_words, 0, 1)
+        load_codes(w_codes[1], w_qkv_words, 1, 1)
+        for n in (2, 3, 4):
+            load_scales(w_planes[n], w_qkv_scales, n)
+        for n in (2, 3, 4):
+            load_codes(w_codes[n], w_qkv_words, n, 1)
+        for c in (1, 2):
+            load_scales(x_planes[c], x_scales, c)
+        for c in (1, 2):
+            load_codes(x_codes[c], x_words, c, 1)
+
+        nc.vector.tensor_copy(out=cos_tab[:, :, :, 0], in_=cos_raw[:])
+        nc.vector.tensor_copy(out=cos_tab[:, :, :, 1], in_=cos_raw[:])
+        nc.vector.tensor_scalar_mul(out=sin_tab[:, :, :, 0], in0=sin_raw[:], scalar1=-1.0)
+        nc.vector.tensor_copy(out=sin_tab[:, :, :, 1], in_=sin_raw[:])
+
+        for c in range(NGROUPS):
+            if c >= 1 and c + 2 < NGROUPS:
+                load_scales(x_planes[c + 2], x_scales, c + 2)
+                load_codes(x_codes[c + 2], x_words, c + 2, 1)
+            rows = slice(P * GROUP * c, P * GROUP * (c + 1))
+            order = ROTATED[: V_PLACE[c]] + (VBLOCK,) + ROTATED[V_PLACE[c] :]
+            last_group = c == NGROUPS - 1
+            for n in order:
+                rotated = n != VBLOCK
+                fine = last_group and n in (4, VBLOCK)
+                if rotated:
+                    direct = work.tile([P, GROUP, BLOCK], F32, name="direct", bufs=6)
+                    crossed = work.tile([P, GROUP, BLOCK], F32, name="crossed", bufs=3)
+                else:
+                    values = work.tile([P, GROUP, BLOCK], F32, name="values", bufs=2)
+                for mi in range(GROUP):
+                    acc = psum.tile([P, BLOCK], F32, name="acc")
+                    for g in range(PASSES):
+                        nc.tensor.matmul_mx(
+                            out=acc[:],
+                            lhsT=x_codes[c][:, g, 2 * P * mi : 2 * P * (mi + 1)].bitcast(FP4X4),
+                            lhsT_scale=x_planes[c][:, g, P * mi : P * (mi + 1)],
+                            rhs=w_codes[n][:, g, :].bitcast(FP4X4),
+                            rhs_scale=w_planes[n][:, g, :],
+                            start=(g == 0),
+                            stop=(g == PASSES - 1),
+                        )
+                    if rotated:
+                        a = (GROUP * c + mi) % POS_TILES
+                        nc.vector.tensor_tensor(
+                            out=direct[:, mi, :].rearrange("p (h d) -> p h d", h=HEADS),
+                            in0=acc[:].rearrange("p (h d) -> p h d", h=HEADS),
+                            in1=cos_tab[:, a].rearrange("p j t -> p (j t)").unsqueeze(1).to_broadcast([P, HEADS, HD]),
+                            op=MULT,
+                        )
+                        nc.vector.tensor_tensor(
+                            out=crossed[:, mi, :].rearrange("p (h j t) -> p h j t", h=HEADS, t=2),
+                            in0=acc[:].rearrange("p (h j t) -> p h j t", h=HEADS, t=2)[:, :, :, ::-1],
+                            in1=sin_tab[:, a].unsqueeze(1).to_broadcast([P, HEADS, HD // 2, 2]),
+                            op=MULT,
+                        )
+                    else:
+                        nc.scalar.copy(out=values[:, mi, :], in_=acc[:])
+                        if fine:
+                            nc.scalar.dma_start(
+                                out=v_rows[rows, :].rearrange("(m p) f -> p m f", p=P)[:, mi, :], in_=values[:, mi, :]
+                            )
+                if rotated:
+                    if n < 4:
+                        dest = q_rows[rows, BLOCK * n : BLOCK * (n + 1)]
+                    else:
+                        dest = k_rows[rows, :]
+                    dest = dest.rearrange("(m p) f -> p m f", p=P)
+                    if fine:
+                        for mi in range(GROUP):
+                            nc.vector.tensor_tensor(
+                                out=direct[:, mi, :], in0=direct[:, mi, :], in1=crossed[:, mi, :], op=ADD
+                            )
+                            nc.sync.dma_start(out=dest[:, mi, :], in_=direct[:, mi, :])
+                    else:
+                        nc.gpsimd.tensor_tensor(out=direct[:], in0=direct[:], in1=crossed[:], op=ADD)
+                        nc.sync.dma_start(out=dest, in_=direct[:])
+                elif not fine:
+                    nc.scalar.dma_start(out=v_rows[rows, :].rearrange("(m p) f -> p m f", p=P), in_=values[:])

@@ -18,6 +18,7 @@ NQ = 2048
 NKV = 512
 NCOLS = NQ + 2 * NKV
 BLOCK = 512
+HALF = BLOCK // 2
 NBLOCKS = NCOLS // BLOCK
 VBLOCK = 5
 GROUP = 4
@@ -26,7 +27,8 @@ HD = 128
 HEADS = BLOCK // HD
 POS_TILES = 1024 // P
 ROTATED = (0, 1, 2, 3, 4)
-V_PLACE = (0, 1, 1, 2, 3, 4, 4, 5)
+V_AFTER = (0, 7, 14, 20, 27, 34, 40, 40)
+WARM = 16
 
 FLOPS = 2 * TOKENS * K * NCOLS
 
@@ -49,10 +51,12 @@ def tile_causalselfattention_pa_kernel(
         x_planes = [keep.tile([P, PASSES, BLOCK], U8, name="xs%d" % c, align_bytes=64) for c in range(NGROUPS)]
         w_codes = [keep.tile([P, PASSES, 2 * BLOCK], U8, name="wc%d" % n, align_bytes=64) for n in range(NBLOCKS)]
         w_planes = [keep.tile([P, PASSES, BLOCK], U8, name="ws%d" % n, align_bytes=64) for n in range(NBLOCKS)]
-        cos_raw = keep.tile([P, POS_TILES, HD // 2], BF16, name="cos_raw")
-        sin_raw = keep.tile([P, POS_TILES, HD // 2], BF16, name="sin_raw")
-        cos_tab = keep.tile([P, POS_TILES, HD // 2, 2], F32, name="cos_tab")
-        sin_tab = keep.tile([P, POS_TILES, HD // 2, 2], F32, name="sin_tab")
+        cos_raw = keep.tile([P, POS_TILES * HD // 2], BF16, name="cos_raw")
+        sin_raw = keep.tile([P, POS_TILES * HD // 2], BF16, name="sin_raw")
+        cos_tab = keep.tile([P, POS_TILES, HD], F32, name="cos_tab")
+        sin_tab = keep.tile([P, POS_TILES, HD], F32, name="sin_tab")
+        signs = keep.tile([P, 2], F32, name="signs")
+        zeros = keep.tile([P, BLOCK], BF16, name="zeros")
 
         def zero_plane(plane):
             nc.vector.memset(plane[:].bitcast(I32), 0)
@@ -66,107 +70,150 @@ def tile_causalselfattention_pa_kernel(
                     .bitcast(I32),
                 )
 
-        def load_codes(codes, words, i, pieces):
-            step = PASSES // pieces
-            for g0 in range(0, PASSES, step):
-                nc.sync.dma_start(
-                    out=codes[:, g0 : g0 + step, :].bitcast(I32),
-                    in_=words[g0 : g0 + step, :, 2 * BLOCK * i : 2 * BLOCK * (i + 1)]
-                    .rearrange("g p b -> p g b")
-                    .bitcast(I32),
-                )
+        def load_codes(codes, words, i, first=0, count=BLOCK):
+            nc.sync.dma_start(
+                out=codes[:, :, 2 * first : 2 * (first + count)].bitcast(I32),
+                in_=words[:, :, 2 * (BLOCK * i + first) : 2 * (BLOCK * i + first + count)]
+                .rearrange("g p b -> p g b")
+                .bitcast(I32),
+            )
+
+        nc.gpsimd.memset(zeros[:], 0.0)
+        warm = psum.tile([P, BLOCK], F32, name="acc")
+        for i in range(WARM):
+            nc.tensor.matmul(out=warm[:], lhsT=zeros[:, :P], rhs=zeros[:], start=True, stop=True)
 
         zero_plane(w_planes[VBLOCK])
         zero_plane(x_planes[0])
         load_scales(w_planes[VBLOCK], w_qkv_scales, VBLOCK)
         load_scales(x_planes[0], x_scales, 0)
-        load_codes(x_codes[0], x_words, 0, 2)
-        load_codes(w_codes[VBLOCK], w_qkv_words, VBLOCK, 2)
-        nc.scalar.dma_start(out=cos_raw[:], in_=freqs_cos.rearrange("(a p) j -> p a j", p=P))
-        nc.scalar.dma_start(out=sin_raw[:], in_=freqs_sin.rearrange("(a p) j -> p a j", p=P))
+        load_codes(w_codes[VBLOCK], w_qkv_words, VBLOCK, 0, HALF)
+        load_codes(x_codes[0], x_words, 0, 0, HALF)
+        load_codes(x_codes[0], x_words, 0, HALF, HALF)
+        load_codes(w_codes[VBLOCK], w_qkv_words, VBLOCK, HALF, HALF)
+        nc.scalar.dma_start(
+            out=cos_raw[:].rearrange("p (a j) -> p a j", a=POS_TILES), in_=freqs_cos.rearrange("(a p) j -> p a j", p=P)
+        )
+        nc.scalar.dma_start(
+            out=sin_raw[:].rearrange("p (a j) -> p a j", a=POS_TILES), in_=freqs_sin.rearrange("(a p) j -> p a j", p=P)
+        )
         for n in range(VBLOCK):
             zero_plane(w_planes[n])
         for c in range(1, NGROUPS):
             zero_plane(x_planes[c])
         load_scales(w_planes[0], w_qkv_scales, 0)
         load_scales(w_planes[1], w_qkv_scales, 1)
-        load_codes(w_codes[0], w_qkv_words, 0, 1)
-        load_codes(w_codes[1], w_qkv_words, 1, 1)
+        load_codes(w_codes[0], w_qkv_words, 0)
+        load_codes(w_codes[1], w_qkv_words, 1)
         for n in (2, 3, 4):
             load_scales(w_planes[n], w_qkv_scales, n)
         for n in (2, 3, 4):
-            load_codes(w_codes[n], w_qkv_words, n, 1)
+            load_codes(w_codes[n], w_qkv_words, n)
         for c in (1, 2):
             load_scales(x_planes[c], x_scales, c)
         for c in (1, 2):
-            load_codes(x_codes[c], x_words, c, 1)
+            load_codes(x_codes[c], x_words, c)
 
-        nc.vector.tensor_copy(out=cos_tab[:, :, :, 0], in_=cos_raw[:])
-        nc.vector.tensor_copy(out=cos_tab[:, :, :, 1], in_=cos_raw[:])
-        nc.vector.tensor_scalar_mul(out=sin_tab[:, :, :, 0], in0=sin_raw[:], scalar1=-1.0)
-        nc.vector.tensor_copy(out=sin_tab[:, :, :, 1], in_=sin_raw[:])
+        pairs = POS_TILES * HD // 2
+        nc.vector.memset(signs[:, 0:1], -1.0)
+        nc.vector.memset(signs[:, 1:2], 1.0)
+        nc.vector.tensor_copy(
+            out=cos_tab[:].rearrange("p a (j t) -> p (a j) t", t=2),
+            in_=cos_raw[:].unsqueeze(2).to_broadcast([P, pairs, 2]),
+        )
+        nc.vector.tensor_tensor(
+            out=sin_tab[:].rearrange("p a (j t) -> p (a j) t", t=2),
+            in0=sin_raw[:].unsqueeze(2).to_broadcast([P, pairs, 2]),
+            in1=signs[:].unsqueeze(1).to_broadcast([P, pairs, 2]),
+            op=MULT,
+        )
 
-        for c in range(NGROUPS):
-            if c >= 1 and c + 2 < NGROUPS:
+        def project(c, mi, n, first, count):
+            acc = psum.tile([P, count], F32, name="acc")
+            for g in range(PASSES):
+                nc.tensor.matmul_mx(
+                    out=acc[:],
+                    lhsT=x_codes[c][:, g, 2 * P * mi : 2 * P * (mi + 1)].bitcast(FP4X4),
+                    lhsT_scale=x_planes[c][:, g, P * mi : P * (mi + 1)],
+                    rhs=w_codes[n][:, g, 2 * first : 2 * (first + count)].bitcast(FP4X4),
+                    rhs_scale=w_planes[n][:, g, first : first + count],
+                    start=(g == 0),
+                    stop=(g == PASSES - 1),
+                )
+            return acc
+
+        blocks = []
+        for r in range(len(ROTATED) * NGROUPS + 1):
+            blocks.extend((c, VBLOCK) for c in range(NGROUPS) if V_AFTER[c] == r)
+            if r < len(ROTATED) * NGROUPS:
+                blocks.append((r // len(ROTATED), ROTATED[r % len(ROTATED)]))
+
+        for b, (c, n) in enumerate(blocks):
+            if n == 0 and c >= 1 and c + 2 < NGROUPS:
                 load_scales(x_planes[c + 2], x_scales, c + 2)
-                load_codes(x_codes[c + 2], x_words, c + 2, 1)
+                load_codes(x_codes[c + 2], x_words, c + 2)
             rows = slice(P * GROUP * c, P * GROUP * (c + 1))
-            order = ROTATED[: V_PLACE[c]] + (VBLOCK,) + ROTATED[V_PLACE[c] :]
-            last_group = c == NGROUPS - 1
-            for n in order:
-                rotated = n != VBLOCK
-                fine = last_group and n in (4, VBLOCK)
-                if rotated:
-                    direct = work.tile([P, GROUP, BLOCK], F32, name="direct", bufs=6)
-                    crossed = work.tile([P, GROUP, BLOCK], F32, name="crossed", bufs=3)
+            fine = b >= len(blocks) - 3
+            if n == VBLOCK:
+                dest = v_rows[rows, :].rearrange("(m p) f -> p m f", p=P)
+                values = work.tile([P, GROUP, BLOCK], F32, name="values", bufs=2)
+                if b == 0:
+                    steps = [(mi, first, HALF) for first in (0, HALF) for mi in range(GROUP)]
+                    steps.append((nc.scalar, 0, GROUP, 0, BLOCK))
+                elif b == len(blocks) - 2:
+                    steps = [(0, 0, BLOCK), (1, 0, BLOCK), (nc.scalar, 0, 2, 0, BLOCK)]
+                    steps += [(2, 0, BLOCK), (3, 0, BLOCK), (nc.scalar, 2, 4, 0, BLOCK)]
+                elif b == len(blocks) - 1:
+                    steps = [(0, 0, BLOCK), (1, 0, BLOCK), (nc.scalar, 0, 2, 0, BLOCK)]
+                    steps += [(2, 0, BLOCK), (nc.sync, 2, 3, 0, BLOCK)]
+                    steps += [(3, 0, HALF), (nc.scalar, 3, 4, 0, HALF)]
+                    steps += [(3, HALF, HALF), (nc.sync, 3, 4, HALF, HALF)]
                 else:
-                    values = work.tile([P, GROUP, BLOCK], F32, name="values", bufs=2)
-                for mi in range(GROUP):
-                    acc = psum.tile([P, BLOCK], F32, name="acc")
-                    for g in range(PASSES):
-                        nc.tensor.matmul_mx(
-                            out=acc[:],
-                            lhsT=x_codes[c][:, g, 2 * P * mi : 2 * P * (mi + 1)].bitcast(FP4X4),
-                            lhsT_scale=x_planes[c][:, g, P * mi : P * (mi + 1)],
-                            rhs=w_codes[n][:, g, :].bitcast(FP4X4),
-                            rhs_scale=w_planes[n][:, g, :],
-                            start=(g == 0),
-                            stop=(g == PASSES - 1),
-                        )
-                    if rotated:
-                        a = (GROUP * c + mi) % POS_TILES
-                        nc.vector.tensor_tensor(
-                            out=direct[:, mi, :].rearrange("p (h d) -> p h d", h=HEADS),
-                            in0=acc[:].rearrange("p (h d) -> p h d", h=HEADS),
-                            in1=cos_tab[:, a].rearrange("p j t -> p (j t)").unsqueeze(1).to_broadcast([P, HEADS, HD]),
-                            op=MULT,
-                        )
-                        nc.vector.tensor_tensor(
-                            out=crossed[:, mi, :].rearrange("p (h j t) -> p h j t", h=HEADS, t=2),
-                            in0=acc[:].rearrange("p (h j t) -> p h j t", h=HEADS, t=2)[:, :, :, ::-1],
-                            in1=sin_tab[:, a].unsqueeze(1).to_broadcast([P, HEADS, HD // 2, 2]),
-                            op=MULT,
-                        )
+                    steps = [(mi, 0, BLOCK) for mi in range(GROUP)]
+                    steps.append((nc.scalar, 0, GROUP, 0, BLOCK))
+                for s, step in enumerate(steps):
+                    if len(step) == 3:
+                        mi, first, count = step
+                        acc = project(c, mi, n, first, count)
+                        if b == len(blocks) - 1 and s == len(steps) - 2:
+                            nc.vector.tensor_copy(out=values[:, mi, first : first + count], in_=acc[:])
+                        else:
+                            nc.scalar.copy(out=values[:, mi, first : first + count], in_=acc[:])
                     else:
-                        nc.scalar.copy(out=values[:, mi, :], in_=acc[:])
-                        if fine:
-                            nc.scalar.dma_start(
-                                out=v_rows[rows, :].rearrange("(m p) f -> p m f", p=P)[:, mi, :], in_=values[:, mi, :]
-                            )
-                if rotated:
-                    if n < 4:
-                        dest = q_rows[rows, BLOCK * n : BLOCK * (n + 1)]
-                    else:
-                        dest = k_rows[rows, :]
-                    dest = dest.rearrange("(m p) f -> p m f", p=P)
-                    if fine:
-                        for mi in range(GROUP):
-                            nc.vector.tensor_tensor(
-                                out=direct[:, mi, :], in0=direct[:, mi, :], in1=crossed[:, mi, :], op=ADD
-                            )
-                            nc.sync.dma_start(out=dest[:, mi, :], in_=direct[:, mi, :])
-                    else:
-                        nc.gpsimd.tensor_tensor(out=direct[:], in0=direct[:], in1=crossed[:], op=ADD)
-                        nc.sync.dma_start(out=dest, in_=direct[:])
-                elif not fine:
-                    nc.scalar.dma_start(out=v_rows[rows, :].rearrange("(m p) f -> p m f", p=P), in_=values[:])
+                        queue, lo, hi, first, count = step
+                        queue.dma_start(
+                            out=dest[:, lo:hi, first : first + count], in_=values[:, lo:hi, first : first + count]
+                        )
+                continue
+
+            if n < 4:
+                dest = q_rows[rows, BLOCK * n : BLOCK * (n + 1)]
+            else:
+                dest = k_rows[rows, :]
+            dest = dest.rearrange("(m p) f -> p m f", p=P)
+            direct = work.tile([P, GROUP, BLOCK], F32, name="direct", bufs=6)
+            crossed = work.tile([P, GROUP, BLOCK], F32, name="crossed", bufs=3)
+            for mi in range(GROUP):
+                acc = project(c, mi, n, 0, BLOCK)
+                a = (GROUP * c + mi) % POS_TILES
+                nc.vector.tensor_tensor(
+                    out=direct[:, mi, :].rearrange("p (h d) -> p h d", h=HEADS),
+                    in0=acc[:].rearrange("p (h d) -> p h d", h=HEADS),
+                    in1=cos_tab[:, a, :].unsqueeze(1).to_broadcast([P, HEADS, HD]),
+                    op=MULT,
+                )
+                nc.vector.tensor_tensor(
+                    out=crossed[:, mi, :].rearrange("p (h j t) -> p h j t", h=HEADS, t=2),
+                    in0=acc[:].rearrange("p (h j t) -> p h j t", h=HEADS, t=2)[:, :, :, ::-1],
+                    in1=sin_tab[:, a, :].rearrange("p (j t) -> p j t", t=2).unsqueeze(1).to_broadcast([P, HEADS, HD // 2, 2]),
+                    op=MULT,
+                )
+            if fine:
+                for lo in range(0, GROUP, 2):
+                    nc.vector.tensor_tensor(
+                        out=direct[:, lo : lo + 2, :], in0=direct[:, lo : lo + 2, :], in1=crossed[:, lo : lo + 2, :], op=ADD
+                    )
+                    nc.sync.dma_start(out=dest[:, lo : lo + 2, :], in_=direct[:, lo : lo + 2, :])
+            else:
+                nc.gpsimd.tensor_tensor(out=direct[:], in0=direct[:], in1=crossed[:], op=ADD)
+                nc.sync.dma_start(out=dest, in_=direct[:])

@@ -26,9 +26,9 @@ NGROUPS = TOKENS // (P * GROUP)
 HD = 128
 HEADS = BLOCK // HD
 POS_TILES = 1024 // P
-ROTATED = (0, 1, 2, 3, 4)
+ROTATED = (4, 0, 1, 2, 3)
 V_AFTER = (0, 7, 14, 20, 27, 34, 40, 40)
-WARM = 16
+WARM = 14
 
 FLOPS = 2 * TOKENS * K * NCOLS
 
@@ -48,9 +48,20 @@ def tile_causalselfattention_pa_kernel(
         ctx.enter_context(tc.manual_schedule())
 
         x_codes = [keep.tile([P, PASSES, 2 * BLOCK], U8, name="xc%d" % c, align_bytes=64) for c in range(NGROUPS)]
-        x_planes = [keep.tile([P, PASSES, BLOCK], U8, name="xs%d" % c, align_bytes=64) for c in range(NGROUPS)]
+        x_sets = ((0, 1), (1, 2), (3, 2), (5, 2), (7, 1))
+        w_sets = ((4, 2), (0, 4))
+        x_plane_tiles = [keep.tile([P, PASSES, BLOCK * k], U8, name="xs%d" % f, align_bytes=64) for f, k in x_sets]
+        w_plane_tiles = [keep.tile([P, PASSES, BLOCK * k], U8, name="ws%d" % f, align_bytes=64) for f, k in w_sets]
+
+        def plane_of(tiles, sets, i):
+            for tile_, (f, k) in zip(tiles, sets):
+                if f <= i < f + k:
+                    return tile_[:, :, BLOCK * (i - f) : BLOCK * (i - f + 1)]
+            return None
+
+        x_planes = [plane_of(x_plane_tiles, x_sets, c) for c in range(NGROUPS)]
+        w_planes = [plane_of(w_plane_tiles, w_sets, n) for n in range(NBLOCKS)]
         w_codes = [keep.tile([P, PASSES, 2 * BLOCK], U8, name="wc%d" % n, align_bytes=64) for n in range(NBLOCKS)]
-        w_planes = [keep.tile([P, PASSES, BLOCK], U8, name="ws%d" % n, align_bytes=64) for n in range(NBLOCKS)]
         cos_raw = keep.tile([P, POS_TILES * HD // 2], BF16, name="cos_raw")
         sin_raw = keep.tile([P, POS_TILES * HD // 2], BF16, name="sin_raw")
         cos_tab = keep.tile([P, POS_TILES, HD], F32, name="cos_tab")
@@ -61,11 +72,12 @@ def tile_causalselfattention_pa_kernel(
         def zero_plane(plane):
             nc.vector.memset(plane[:].bitcast(I32), 0)
 
-        def load_scales(plane, scales, i):
+        def load_scales(plane, scales, first_and_blocks):
+            f, k = first_and_blocks
             for quad in range(4):
                 nc.sync.dma_start(
                     out=plane[32 * quad : 32 * quad + 4, :, :].bitcast(I32),
-                    in_=scales[:, 4 * quad : 4 * quad + 4, BLOCK * i : BLOCK * (i + 1)]
+                    in_=scales[:, 4 * quad : 4 * quad + 4, BLOCK * f : BLOCK * (f + k)]
                     .rearrange("g r n -> r g n")
                     .bitcast(I32),
                 )
@@ -83,50 +95,46 @@ def tile_causalselfattention_pa_kernel(
         for i in range(WARM):
             nc.tensor.matmul(out=warm[:], lhsT=zeros[:, :P], rhs=zeros[:], start=True, stop=True)
 
-        zero_plane(w_planes[VBLOCK])
-        zero_plane(x_planes[0])
-        load_scales(w_planes[VBLOCK], w_qkv_scales, VBLOCK)
-        load_scales(x_planes[0], x_scales, 0)
         load_codes(w_codes[VBLOCK], w_qkv_words, VBLOCK, 0, HALF)
         load_codes(x_codes[0], x_words, 0, 0, HALF)
+        zero_plane(w_plane_tiles[0])
+        zero_plane(x_plane_tiles[0])
+        load_scales(w_plane_tiles[0], w_qkv_scales, w_sets[0])
+        load_scales(x_plane_tiles[0], x_scales, x_sets[0])
         load_codes(x_codes[0], x_words, 0, HALF, HALF)
         load_codes(w_codes[VBLOCK], w_qkv_words, VBLOCK, HALF, HALF)
+        load_codes(w_codes[4], w_qkv_words, 4)
         nc.scalar.dma_start(
             out=cos_raw[:].rearrange("p (a j) -> p a j", a=POS_TILES), in_=freqs_cos.rearrange("(a p) j -> p a j", p=P)
         )
         nc.scalar.dma_start(
             out=sin_raw[:].rearrange("p (a j) -> p a j", a=POS_TILES), in_=freqs_sin.rearrange("(a p) j -> p a j", p=P)
         )
-        for n in range(VBLOCK):
-            zero_plane(w_planes[n])
-        for c in range(1, NGROUPS):
-            zero_plane(x_planes[c])
-        load_scales(w_planes[0], w_qkv_scales, 0)
-        load_scales(w_planes[1], w_qkv_scales, 1)
-        load_codes(w_codes[0], w_qkv_words, 0)
-        load_codes(w_codes[1], w_qkv_words, 1)
-        for n in (2, 3, 4):
-            load_scales(w_planes[n], w_qkv_scales, n)
-        for n in (2, 3, 4):
+        zero_plane(w_plane_tiles[1])
+        for tile_ in x_plane_tiles[1:]:
+            zero_plane(tile_)
+        load_scales(w_plane_tiles[1], w_qkv_scales, w_sets[1])
+        for n in (0, 1, 2, 3):
             load_codes(w_codes[n], w_qkv_words, n)
-        for c in (1, 2):
-            load_scales(x_planes[c], x_scales, c)
+        load_scales(x_plane_tiles[1], x_scales, x_sets[1])
         for c in (1, 2):
             load_codes(x_codes[c], x_words, c)
 
-        pairs = POS_TILES * HD // 2
         nc.vector.memset(signs[:, 0:1], -1.0)
         nc.vector.memset(signs[:, 1:2], 1.0)
-        nc.vector.tensor_copy(
-            out=cos_tab[:].rearrange("p a (j t) -> p (a j) t", t=2),
-            in_=cos_raw[:].unsqueeze(2).to_broadcast([P, pairs, 2]),
-        )
-        nc.vector.tensor_tensor(
-            out=sin_tab[:].rearrange("p a (j t) -> p (a j) t", t=2),
-            in0=sin_raw[:].unsqueeze(2).to_broadcast([P, pairs, 2]),
-            in1=signs[:].unsqueeze(1).to_broadcast([P, pairs, 2]),
-            op=MULT,
-        )
+        pairs = GROUP * HD // 2
+        for a0 in range(0, POS_TILES, GROUP):
+            raw = slice(a0 * HD // 2, a0 * HD // 2 + pairs)
+            nc.vector.tensor_copy(
+                out=cos_tab[:, a0 : a0 + GROUP, :].rearrange("p a (j t) -> p (a j) t", t=2),
+                in_=cos_raw[:, raw].unsqueeze(2).to_broadcast([P, pairs, 2]),
+            )
+            nc.vector.tensor_tensor(
+                out=sin_tab[:, a0 : a0 + GROUP, :].rearrange("p a (j t) -> p (a j) t", t=2),
+                in0=sin_raw[:, raw].unsqueeze(2).to_broadcast([P, pairs, 2]),
+                in1=signs[:].unsqueeze(1).to_broadcast([P, pairs, 2]),
+                op=MULT,
+            )
 
         def project(c, mi, n, first, count):
             acc = psum.tile([P, count], F32, name="acc")
@@ -147,11 +155,14 @@ def tile_causalselfattention_pa_kernel(
             blocks.extend((c, VBLOCK) for c in range(NGROUPS) if V_AFTER[c] == r)
             if r < len(ROTATED) * NGROUPS:
                 blocks.append((r // len(ROTATED), ROTATED[r % len(ROTATED)]))
+        prefetch = {(1, ROTATED[0]): 2, (3, ROTATED[0]): 3, (5, ROTATED[0]): 4}
 
         for b, (c, n) in enumerate(blocks):
-            if n == 0 and c >= 1 and c + 2 < NGROUPS:
-                load_scales(x_planes[c + 2], x_scales, c + 2)
-                load_codes(x_codes[c + 2], x_words, c + 2)
+            if (c, n) in prefetch:
+                s = prefetch[(c, n)]
+                load_scales(x_plane_tiles[s], x_scales, x_sets[s])
+                for c2 in range(x_sets[s][0], x_sets[s][0] + x_sets[s][1]):
+                    load_codes(x_codes[c2], x_words, c2)
             rows = slice(P * GROUP * c, P * GROUP * (c + 1))
             fine = b >= len(blocks) - 3
             if n == VBLOCK:

@@ -26,9 +26,9 @@ NGROUPS = TOKENS // (P * GROUP)
 HD = 128
 HEADS = BLOCK // HD
 POS_TILES = 1024 // P
-ROTATED = (4, 0, 1, 2, 3)
+ROTATED = (0, 1, 2, 3, 4)
 V_AFTER = (0, 7, 14, 20, 27, 34, 40, 40)
-WARM = 14
+WARM = 20
 
 FLOPS = 2 * TOKENS * K * NCOLS
 
@@ -48,20 +48,9 @@ def tile_causalselfattention_pa_kernel(
         ctx.enter_context(tc.manual_schedule())
 
         x_codes = [keep.tile([P, PASSES, 2 * BLOCK], U8, name="xc%d" % c, align_bytes=64) for c in range(NGROUPS)]
-        x_sets = ((0, 1), (1, 2), (3, 2), (5, 2), (7, 1))
-        w_sets = ((4, 2), (0, 4))
-        x_plane_tiles = [keep.tile([P, PASSES, BLOCK * k], U8, name="xs%d" % f, align_bytes=64) for f, k in x_sets]
-        w_plane_tiles = [keep.tile([P, PASSES, BLOCK * k], U8, name="ws%d" % f, align_bytes=64) for f, k in w_sets]
-
-        def plane_of(tiles, sets, i):
-            for tile_, (f, k) in zip(tiles, sets):
-                if f <= i < f + k:
-                    return tile_[:, :, BLOCK * (i - f) : BLOCK * (i - f + 1)]
-            return None
-
-        x_planes = [plane_of(x_plane_tiles, x_sets, c) for c in range(NGROUPS)]
-        w_planes = [plane_of(w_plane_tiles, w_sets, n) for n in range(NBLOCKS)]
+        x_planes = [keep.tile([P, PASSES, BLOCK], U8, name="xs%d" % c, align_bytes=64) for c in range(NGROUPS)]
         w_codes = [keep.tile([P, PASSES, 2 * BLOCK], U8, name="wc%d" % n, align_bytes=64) for n in range(NBLOCKS)]
+        w_planes = [keep.tile([P, PASSES, BLOCK], U8, name="ws%d" % n, align_bytes=64) for n in range(NBLOCKS)]
         cos_raw = keep.tile([P, POS_TILES * HD // 2], BF16, name="cos_raw")
         sin_raw = keep.tile([P, POS_TILES * HD // 2], BF16, name="sin_raw")
         cos_tab = keep.tile([P, POS_TILES, HD], F32, name="cos_tab")
@@ -72,12 +61,11 @@ def tile_causalselfattention_pa_kernel(
         def zero_plane(plane):
             nc.vector.memset(plane[:].bitcast(I32), 0)
 
-        def load_scales(plane, scales, first_and_blocks):
-            f, k = first_and_blocks
+        def load_scales(plane, scales, i):
             for quad in range(4):
                 nc.sync.dma_start(
                     out=plane[32 * quad : 32 * quad + 4, :, :].bitcast(I32),
-                    in_=scales[:, 4 * quad : 4 * quad + 4, BLOCK * f : BLOCK * (f + k)]
+                    in_=scales[:, 4 * quad : 4 * quad + 4, BLOCK * i : BLOCK * (i + 1)]
                     .rearrange("g r n -> r g n")
                     .bitcast(I32),
                 )
@@ -95,46 +83,50 @@ def tile_causalselfattention_pa_kernel(
         for i in range(WARM):
             nc.tensor.matmul(out=warm[:], lhsT=zeros[:, :P], rhs=zeros[:], start=True, stop=True)
 
+        zero_plane(w_planes[VBLOCK])
+        zero_plane(x_planes[0])
+        load_scales(w_planes[VBLOCK], w_qkv_scales, VBLOCK)
+        load_scales(x_planes[0], x_scales, 0)
         load_codes(w_codes[VBLOCK], w_qkv_words, VBLOCK, 0, HALF)
         load_codes(x_codes[0], x_words, 0, 0, HALF)
-        zero_plane(w_plane_tiles[0])
-        zero_plane(x_plane_tiles[0])
-        load_scales(w_plane_tiles[0], w_qkv_scales, w_sets[0])
-        load_scales(x_plane_tiles[0], x_scales, x_sets[0])
         load_codes(x_codes[0], x_words, 0, HALF, HALF)
         load_codes(w_codes[VBLOCK], w_qkv_words, VBLOCK, HALF, HALF)
-        load_codes(w_codes[4], w_qkv_words, 4)
         nc.scalar.dma_start(
             out=cos_raw[:].rearrange("p (a j) -> p a j", a=POS_TILES), in_=freqs_cos.rearrange("(a p) j -> p a j", p=P)
         )
         nc.scalar.dma_start(
             out=sin_raw[:].rearrange("p (a j) -> p a j", a=POS_TILES), in_=freqs_sin.rearrange("(a p) j -> p a j", p=P)
         )
-        zero_plane(w_plane_tiles[1])
-        for tile_ in x_plane_tiles[1:]:
-            zero_plane(tile_)
-        load_scales(w_plane_tiles[1], w_qkv_scales, w_sets[1])
-        for n in (0, 1, 2, 3):
+        for n in range(VBLOCK):
+            zero_plane(w_planes[n])
+        for c in range(1, NGROUPS):
+            zero_plane(x_planes[c])
+        load_scales(w_planes[0], w_qkv_scales, 0)
+        load_scales(w_planes[1], w_qkv_scales, 1)
+        load_codes(w_codes[0], w_qkv_words, 0)
+        load_codes(w_codes[1], w_qkv_words, 1)
+        for n in (2, 3, 4):
+            load_scales(w_planes[n], w_qkv_scales, n)
+        for n in (2, 3, 4):
             load_codes(w_codes[n], w_qkv_words, n)
-        load_scales(x_plane_tiles[1], x_scales, x_sets[1])
+        for c in (1, 2):
+            load_scales(x_planes[c], x_scales, c)
         for c in (1, 2):
             load_codes(x_codes[c], x_words, c)
 
+        pairs = POS_TILES * HD // 2
         nc.vector.memset(signs[:, 0:1], -1.0)
         nc.vector.memset(signs[:, 1:2], 1.0)
-        pairs = GROUP * HD // 2
-        for a0 in range(0, POS_TILES, GROUP):
-            raw = slice(a0 * HD // 2, a0 * HD // 2 + pairs)
-            nc.vector.tensor_copy(
-                out=cos_tab[:, a0 : a0 + GROUP, :].rearrange("p a (j t) -> p (a j) t", t=2),
-                in_=cos_raw[:, raw].unsqueeze(2).to_broadcast([P, pairs, 2]),
-            )
-            nc.vector.tensor_tensor(
-                out=sin_tab[:, a0 : a0 + GROUP, :].rearrange("p a (j t) -> p (a j) t", t=2),
-                in0=sin_raw[:, raw].unsqueeze(2).to_broadcast([P, pairs, 2]),
-                in1=signs[:].unsqueeze(1).to_broadcast([P, pairs, 2]),
-                op=MULT,
-            )
+        nc.vector.tensor_copy(
+            out=cos_tab[:].rearrange("p a (j t) -> p (a j) t", t=2),
+            in_=cos_raw[:].unsqueeze(2).to_broadcast([P, pairs, 2]),
+        )
+        nc.vector.tensor_tensor(
+            out=sin_tab[:].rearrange("p a (j t) -> p (a j) t", t=2),
+            in0=sin_raw[:].unsqueeze(2).to_broadcast([P, pairs, 2]),
+            in1=signs[:].unsqueeze(1).to_broadcast([P, pairs, 2]),
+            op=MULT,
+        )
 
         def project(c, mi, n, first, count):
             acc = psum.tile([P, count], F32, name="acc")
@@ -155,14 +147,11 @@ def tile_causalselfattention_pa_kernel(
             blocks.extend((c, VBLOCK) for c in range(NGROUPS) if V_AFTER[c] == r)
             if r < len(ROTATED) * NGROUPS:
                 blocks.append((r // len(ROTATED), ROTATED[r % len(ROTATED)]))
-        prefetch = {(1, ROTATED[0]): 2, (3, ROTATED[0]): 3, (5, ROTATED[0]): 4}
 
         for b, (c, n) in enumerate(blocks):
-            if (c, n) in prefetch:
-                s = prefetch[(c, n)]
-                load_scales(x_plane_tiles[s], x_scales, x_sets[s])
-                for c2 in range(x_sets[s][0], x_sets[s][0] + x_sets[s][1]):
-                    load_codes(x_codes[c2], x_words, c2)
+            if n == 0 and c >= 1 and c + 2 < NGROUPS:
+                load_scales(x_planes[c + 2], x_scales, c + 2)
+                load_codes(x_codes[c + 2], x_words, c + 2)
             rows = slice(P * GROUP * c, P * GROUP * (c + 1))
             fine = b >= len(blocks) - 3
             if n == VBLOCK:

from contextlib import ExitStack

import concourse.mybir as mybir

F32 = mybir.dt.float32
BF16 = mybir.dt.bfloat16
I32 = mybir.dt.int32
U8 = mybir.dt.uint8
FP4X4 = mybir.dt.float4_e2m1fn_x4
MULT = mybir.AluOpType.mult
ADD = mybir.AluOpType.add

P = 128
TOKENS = 4096
K = 2048
PASSES = K // 512
NQ = 2048
NKV = 512
NCOLS = NQ + 2 * NKV
BLOCK = 512
HALF = BLOCK // 2
NBLOCKS = NCOLS // BLOCK
VBLOCK = 5
GROUP = 4
NGROUPS = TOKENS // (P * GROUP)
HD = 128
HEADS = BLOCK // HD
POS_TILES = 1024 // P
ROTATED = (0, 1, 2, 3, 4)
V_AFTER = (0, 7, 14, 20, 27, 34, 40, 40)
WARM = 20

FLOPS = 2 * TOKENS * K * NCOLS


def tile_causalselfattention_pa_kernel(
    tc, x_words, x_scales, w_qkv_words, w_qkv_scales, freqs_cos, freqs_sin, out_0, out_1, out_2
):
    nc = tc.nc
    q_rows = out_0.rearrange("b t h d -> (b t) (h d)")
    k_rows = out_1.rearrange("b t h d -> (b t) (h d)")
    v_rows = out_2.rearrange("b t h d -> (b t) (h d)")

    with ExitStack() as ctx:
        keep = ctx.enter_context(tc.tile_pool(name="keep", bufs=1))
        work = ctx.enter_context(tc.tile_pool(name="work", bufs=1))
        psum = ctx.enter_context(tc.psum_pool(name="psum", bufs=8))
        ctx.enter_context(tc.manual_schedule())

        x_codes = [keep.tile([P, PASSES, 2 * BLOCK], U8, name="xc%d" % c, align_bytes=64) for c in range(NGROUPS)]
        x_planes = [keep.tile([P, PASSES, BLOCK], U8, name="xs%d" % c, align_bytes=64) for c in range(NGROUPS)]
        w_codes = [keep.tile([P, PASSES, 2 * BLOCK], U8, name="wc%d" % n, align_bytes=64) for n in range(NBLOCKS)]
        w_planes = [keep.tile([P, PASSES, BLOCK], U8, name="ws%d" % n, align_bytes=64) for n in range(NBLOCKS)]
        cos_raw = keep.tile([P, POS_TILES * HD // 2], BF16, name="cos_raw")
        sin_raw = keep.tile([P, POS_TILES * HD // 2], BF16, name="sin_raw")
        cos_tab = keep.tile([P, POS_TILES, HD], F32, name="cos_tab")
        sin_tab = keep.tile([P, POS_TILES, HD], F32, name="sin_tab")
        signs = keep.tile([P, 2], F32, name="signs")
        zeros = keep.tile([P, BLOCK], BF16, name="zeros")

        def zero_plane(plane):
            nc.vector.memset(plane[:].bitcast(I32), 0)

        def load_scales(plane, scales, i):
            for quad in range(4):
                nc.sync.dma_start(
                    out=plane[32 * quad : 32 * quad + 4, :, :].bitcast(I32),
                    in_=scales[:, 4 * quad : 4 * quad + 4, BLOCK * i : BLOCK * (i + 1)]
                    .rearrange("g r n -> r g n")
                    .bitcast(I32),
                )

        def load_codes(codes, words, i, first=0, count=BLOCK):
            nc.sync.dma_start(
                out=codes[:, :, 2 * first : 2 * (first + count)].bitcast(I32),
                in_=words[:, :, 2 * (BLOCK * i + first) : 2 * (BLOCK * i + first + count)]
                .rearrange("g p b -> p g b")
                .bitcast(I32),
            )

        nc.gpsimd.memset(zeros[:], 0.0)
        warm = psum.tile([P, BLOCK], F32, name="acc")
        for i in range(WARM):
            nc.tensor.matmul(out=warm[:], lhsT=zeros[:, :P], rhs=zeros[:], start=True, stop=True)

        zero_plane(w_planes[VBLOCK])
        zero_plane(x_planes[0])
        load_scales(w_planes[VBLOCK], w_qkv_scales, VBLOCK)
        load_scales(x_planes[0], x_scales, 0)
        load_codes(w_codes[VBLOCK], w_qkv_words, VBLOCK, 0, HALF)
        load_codes(x_codes[0], x_words, 0, 0, HALF)
        load_codes(x_codes[0], x_words, 0, HALF, HALF)
        load_codes(w_codes[VBLOCK], w_qkv_words, VBLOCK, HALF, HALF)
        nc.scalar.dma_start(
            out=cos_raw[:].rearrange("p (a j) -> p a j", a=POS_TILES), in_=freqs_cos.rearrange("(a p) j -> p a j", p=P)
        )
        nc.scalar.dma_start(
            out=sin_raw[:].rearrange("p (a j) -> p a j", a=POS_TILES), in_=freqs_sin.rearrange("(a p) j -> p a j", p=P)
        )
        for n in range(VBLOCK):
            zero_plane(w_planes[n])
        for c in range(1, NGROUPS):
            zero_plane(x_planes[c])
        load_scales(w_planes[0], w_qkv_scales, 0)
        load_scales(w_planes[1], w_qkv_scales, 1)
        load_codes(w_codes[0], w_qkv_words, 0)
        load_codes(w_codes[1], w_qkv_words, 1)
        for n in (2, 3, 4):
            load_scales(w_planes[n], w_qkv_scales, n)
        for n in (2, 3, 4):
            load_codes(w_codes[n], w_qkv_words, n)
        for c in (1, 2):
            load_scales(x_planes[c], x_scales, c)
        for c in (1, 2):
            load_codes(x_codes[c], x_words, c)

        pairs = POS_TILES * HD // 2
        nc.vector.memset(signs[:, 0:1], -1.0)
        nc.vector.memset(signs[:, 1:2], 1.0)
        nc.vector.tensor_copy(
            out=cos_tab[:].rearrange("p a (j t) -> p (a j) t", t=2),
            in_=cos_raw[:].unsqueeze(2).to_broadcast([P, pairs, 2]),
        )
        nc.vector.tensor_tensor(
            out=sin_tab[:].rearrange("p a (j t) -> p (a j) t", t=2),
            in0=sin_raw[:].unsqueeze(2).to_broadcast([P, pairs, 2]),
            in1=signs[:].unsqueeze(1).to_broadcast([P, pairs, 2]),
            op=MULT,
        )

        def project(c, mi, n, first, count):
            acc = psum.tile([P, count], F32, name="acc")
            for g in range(PASSES):
                nc.tensor.matmul_mx(
                    out=acc[:],
                    lhsT=x_codes[c][:, g, 2 * P * mi : 2 * P * (mi + 1)].bitcast(FP4X4),
                    lhsT_scale=x_planes[c][:, g, P * mi : P * (mi + 1)],
                    rhs=w_codes[n][:, g, 2 * first : 2 * (first + count)].bitcast(FP4X4),
                    rhs_scale=w_planes[n][:, g, first : first + count],
                    start=(g == 0),
                    stop=(g == PASSES - 1),
                )
            return acc

        blocks = []
        for r in range(len(ROTATED) * NGROUPS + 1):
            blocks.extend((c, VBLOCK) for c in range(NGROUPS) if V_AFTER[c] == r)
            if r < len(ROTATED) * NGROUPS:
                blocks.append((r // len(ROTATED), ROTATED[r % len(ROTATED)]))

        for b, (c, n) in enumerate(blocks):
            if n == 0 and c >= 1 and c + 2 < NGROUPS:
                load_scales(x_planes[c + 2], x_scales, c + 2)
                load_codes(x_codes[c + 2], x_words, c + 2)
            rows = slice(P * GROUP * c, P * GROUP * (c + 1))
            fine = b >= len(blocks) - 3
            if n == VBLOCK:
                dest = v_rows[rows, :].rearrange("(m p) f -> p m f", p=P)
                values = work.tile([P, GROUP, BLOCK], F32, name="values", bufs=2)
                if b == 0:
                    steps = [(mi, first, HALF) for first in (0, HALF) for mi in range(GROUP)]
                    steps.append((nc.scalar, 0, GROUP, 0, BLOCK))
                elif b == len(blocks) - 2:
                    steps = [(0, 0, BLOCK), (1, 0, BLOCK), (nc.scalar, 0, 2, 0, BLOCK)]
                    steps += [(2, 0, BLOCK), (3, 0, BLOCK), (nc.scalar, 2, 4, 0, BLOCK)]
                elif b == len(blocks) - 1:
                    steps = [(0, 0, BLOCK), (1, 0, BLOCK), (nc.scalar, 0, 2, 0, BLOCK)]
                    steps += [(2, 0, BLOCK), (nc.sync, 2, 3, 0, BLOCK)]
                    steps += [(3, 0, HALF), (nc.scalar, 3, 4, 0, HALF)]
                    steps += [(3, HALF, HALF), (nc.sync, 3, 4, HALF, HALF)]
                else:
                    steps = [(mi, 0, BLOCK) for mi in range(GROUP)]
                    steps.append((nc.scalar, 0, GROUP, 0, BLOCK))
                for s, step in enumerate(steps):
                    if len(step) == 3:
                        mi, first, count = step
                        acc = project(c, mi, n, first, count)
                        if b == len(blocks) - 1 and s == len(steps) - 2:
                            nc.vector.tensor_copy(out=values[:, mi, first : first + count], in_=acc[:])
                        else:
                            nc.scalar.copy(out=values[:, mi, first : first + count], in_=acc[:])
                    else:
                        queue, lo, hi, first, count = step
                        queue.dma_start(
                            out=dest[:, lo:hi, first : first + count], in_=values[:, lo:hi, first : first + count]
                        )
                continue

            if n < 4:
                dest = q_rows[rows, BLOCK * n : BLOCK * (n + 1)]
            else:
                dest = k_rows[rows, :]
            dest = dest.rearrange("(m p) f -> p m f", p=P)
            direct = work.tile([P, GROUP, BLOCK], F32, name="direct", bufs=6)
            crossed = work.tile([P, GROUP, BLOCK], F32, name="crossed", bufs=3)
            for mi in range(GROUP):
                acc = project(c, mi, n, 0, BLOCK)
                a = (GROUP * c + mi) % POS_TILES
                nc.vector.tensor_tensor(
                    out=direct[:, mi, :].rearrange("p (h d) -> p h d", h=HEADS),
                    in0=acc[:].rearrange("p (h d) -> p h d", h=HEADS),
                    in1=cos_tab[:, a, :].unsqueeze(1).to_broadcast([P, HEADS, HD]),
                    op=MULT,
                )
                nc.vector.tensor_tensor(
                    out=crossed[:, mi, :].rearrange("p (h j t) -> p h j t", h=HEADS, t=2),
                    in0=acc[:].rearrange("p (h j t) -> p h j t", h=HEADS, t=2)[:, :, :, ::-1],
                    in1=sin_tab[:, a, :].rearrange("p (j t) -> p j t", t=2).unsqueeze(1).to_broadcast([P, HEADS, HD // 2, 2]),
                    op=MULT,
                )
            if fine:
                for lo in range(0, GROUP, 2):
                    nc.vector.tensor_tensor(
                        out=direct[:, lo : lo + 2, :], in0=direct[:, lo : lo + 2, :], in1=crossed[:, lo : lo + 2, :], op=ADD
                    )
                    nc.sync.dma_start(out=dest[:, lo : lo + 2, :], in_=direct[:, lo : lo + 2, :])
            else:
                nc.gpsimd.tensor_tensor(out=direct[:], in0=direct[:], in1=crossed[:], op=ADD)
                nc.sync.dma_start(out=dest, in_=direct[:])
